import numpy as np
import ml_dtypes


def mxq(x, axis, fmt="e4m3"):
    dtype, down = {"e4m3": (ml_dtypes.float8_e4m3fn, 7), "e5m2": (ml_dtypes.float8_e5m2, 14)}[fmt]
    v = np.moveaxis(np.asarray(x, np.float32).astype(ml_dtypes.bfloat16).astype(np.float64), axis, -1)
    blocks = v.reshape(v.shape[:-1] + (-1, 32))
    amax = np.abs(blocks).max(-1, keepdims=True)
    byte = np.maximum(np.where(amax > 0, np.frexp(amax)[1] - 1 + 127, 0) - down, 1)
    scale = np.exp2(byte - 127.0)
    codes = (blocks / scale).astype(np.float32).astype(dtype).astype(np.float64)
    return np.moveaxis((codes * scale).reshape(v.shape), -1, axis)


WIDE = False


def mx_kscale(k):
    if not WIDE:
        return np.ones(k)
    levels = np.array([10, -10, 5, -5, 0])
    if k % 512:
        return np.exp2(np.random.permutation(np.resize(levels, k // 32))).repeat(32)
    a = np.empty((k // 512, 16))
    for p in range(k // 512):
        a[p, :8] = np.random.permutation(np.resize(levels, 8))
        for g in range(8):
            far = levels[np.abs(levels - a[p, g]) >= 10]
            a[p, g + 8] = far[np.random.randint(len(far))]
    return np.exp2(a.ravel()).repeat(32)


BF16 = ml_dtypes.bfloat16


def bf(x):
    return np.asarray(x, np.float32).astype(BF16)


def f64(x):
    return np.asarray(x).astype(np.float64)


B, N, C, O = 2, 512, 512, 256
G = 3 * C


def setup_inputs():
    s, t = mx_kscale(N), mx_kscale(C)
    return {"adjacent": bf(np.random.random((B, N, N)) * np.sqrt(3.0 / N) * s),
            "annotations": bf(np.random.standard_normal((B, N, C)) / s[:, None] * t),
            "gc_bias": bf(np.random.standard_normal((1, 1, C)) * 0.3 * t),
            "gru_W": bf(np.random.standard_normal((C, G)) / np.sqrt(C) / t[:, None]),
            "gru_b_x": bf(np.random.standard_normal(G) * 0.3)}


def reference(adjacent, annotations, gc_bias, gru_W, gru_b_x):
    msg = (mxq(f64(adjacent), 2, "e4m3") @ mxq(f64(annotations), 1, "e4m3")) + f64(gc_bias)
    x = msg.reshape(-1, C)
    return (mxq(x, 1, "e4m3") @ mxq(f64(gru_W), 0, "e4m3")) + f64(gru_b_x)

@@ -1,0 +1,297 @@
+from contextlib import ExitStack
+
+import concourse.masks as masks
+import concourse.mybir as mybir
+
+F32 = mybir.dt.float32
+BF16 = mybir.dt.bfloat16
+U32 = mybir.dt.uint32
+U8 = mybir.dt.uint8
+FP8X4 = mybir.dt.float8_e4m3fn_x4
+ADD = mybir.AluOpType.add
+MULT = mybir.AluOpType.mult
+IDENTITY = mybir.ActivationFunctionType.Identity
+
+P = 128
+PACK = 4
+GRAPHS, NODES, CHANNELS, GATES = 2, 512, 512, 1536
+NODE_TILES = NODES // P
+CHANNEL_TILES = CHANNELS // P
+BANK = 512
+GATE_TILES = GATES // BANK
+HALF = 256
+BIAS_COLS = GATES // P
+AHEAD = 2
+
+FLOPS = 2 * GRAPHS * NODES * NODES * CHANNELS + 2 * GRAPHS * NODES * CHANNELS * GATES
+
+
+def tile_gatedgraphconvolution_pa_kernel(tc, adjacent, annotations, gc_bias, gru_W, gru_b_x, out):
+    nc = tc.nc
+    with ExitStack() as ctx:
+        sbuf = ctx.enter_context(tc.tile_pool(name="sbuf", bufs=1))
+        psum_transposes = ctx.enter_context(tc.psum_pool(name="psum_transposes", bufs=2))
+        psum_stage1 = ctx.enter_context(tc.psum_pool(name="psum_stage1", bufs=2))
+        psum_stage2 = ctx.enter_context(tc.psum_pool(name="psum_stage2", bufs=4))
+        ctx.enter_context(tc.manual_schedule())
+
+        def operand(name, columns):
+            grouped = sbuf.tile([P, PACK * columns], BF16, name=name + "_grouped", align_bytes=64)
+            words = sbuf.tile([P, columns], U32, name=name + "_words", align_bytes=64)
+            scales = sbuf.tile([P, columns], U8, name=name + "_scales", align_bytes=64)
+            return grouped, words, scales
+
+        adj_rows = [sbuf.tile([P, NODE_TILES * NODES], BF16, name="adj_rows%d" % b) for b in range(GRAPHS)]
+        ann_planes = [sbuf.tile([P, PACK * CHANNELS], BF16, name="ann_planes%d" % b) for b in range(GRAPHS)]
+        w_planes = [sbuf.tile([P, PACK * BANK], BF16, name="w_planes%d" % g) for g in range(GATE_TILES)]
+        msg_planes = sbuf.tile([P, PACK * NODES], BF16, name="msg_planes")
+        adj = [operand("adj%d" % b, NODES) for b in range(GRAPHS)]
+        ann = [operand("ann%d" % b, CHANNELS) for b in range(GRAPHS)]
+        msg = [operand("msg%d" % b, NODES) for b in range(GRAPHS)]
+        w = [operand("w%d" % g, BANK) for g in range(GATE_TILES)]
+        identity_f32 = sbuf.tile([P, P], F32, name="identity_f32")
+        identity_bf16 = sbuf.tile([P, P], BF16, name="identity_bf16")
+        gc_bf16 = sbuf.tile([P, CHANNEL_TILES], BF16, name="gc_bf16")
+        gc_f32 = sbuf.tile([P, CHANNEL_TILES], F32, name="gc_f32")
+        gate_bias_cols = sbuf.tile([P, BIAS_COLS], BF16, name="gate_bias_cols")
+        gate_bias = sbuf.tile([P, GATES], F32, name="gate_bias")
+        result = sbuf.tile([P, GRAPHS * NODE_TILES * GATES], F32, name="result")
+        out_tiles = out.rearrange("(b p r) g -> b r p g", b=GRAPHS, r=NODE_TILES)
+        in_psum = {}
+
+        def quantise(mx_operand, first, count):
+            grouped, words, scales = mx_operand
+            nc.vector.quantize_mx(
+                out=words[:, first : first + count].bitcast(FP8X4),
+                scales=scales[:, first : first + count],
+                in_=grouped[:, PACK * first : PACK * (first + count)],
+            )
+
+        def regroup(copy, mx_operand, planes, first, count):
+            dst = mx_operand[0][:].rearrange("p (c i t) -> p c t i", i=4, t=PACK)
+            src = planes[:].rearrange("p (t c i) -> p c t i", t=PACK, i=4)
+            copy(out=dst[:, first // 4 : (first + count) // 4], in_=src[:, first // 4 : (first + count) // 4])
+
+        def regroup_annotations(copy, b, half):
+            dst = ann[b][0][:].rearrange("q (t i j) -> q t i j", t=CHANNEL_TILES, j=PACK)
+            src = ann_planes[b][:].rearrange("q (j i t) -> q t i j", j=PACK, t=CHANNEL_TILES)
+            copy(out=dst[:, 2 * half : 2 * half + 2], in_=src[:, 2 * half : 2 * half + 2])
+
+        def gpsimd_copy(out, in_):
+            nc.gpsimd.tensor_scalar(out=out, in0=in_, scalar1=1.0, scalar2=0.0, op0=MULT, op1=ADD)
+
+        def mx_pass(acc, stationary, stationary_first, moving, moving_first, moving_count):
+            rows = slice(stationary_first, stationary_first + P)
+            cols = slice(moving_first, moving_first + moving_count)
+            nc.tensor.matmul_mx(
+                out=acc,
+                lhsT=stationary[1][:, rows].bitcast(FP8X4),
+                lhsT_scale=stationary[2][:, rows],
+                rhs=moving[1][:, cols].bitcast(FP8X4),
+                rhs_scale=moving[2][:, cols],
+                start=True,
+                stop=True,
+            )
+
+        def load_adjacent(b, first_tile, tiles):
+            cols = slice(first_tile * NODES, (first_tile + tiles) * NODES)
+            nc.sync.dma_start(out=adj_rows[b][:, cols], in_=adjacent[b].rearrange("(p r) m -> p (r m)", r=NODE_TILES)[:, cols])
+
+        def load_annotations(b):
+            nc.sync.dma_start(out=ann_planes[b][:], in_=annotations[b].rearrange("(q j) c -> q (j c)", j=PACK))
+
+        def load_weights(g):
+            nc.sync.dma_start(
+                out=w_planes[g][:].rearrange("p (t x) -> p t x", t=PACK),
+                in_=gru_W[:, BANK * g : BANK * (g + 1)].rearrange("(p t) x -> p t x", t=PACK),
+            )
+
+        def spread_gate_bias(block):
+            spread = psum_stage2.tile([P, 4, P], F32, name="acc")
+            for i in range(4):
+                x = 4 * block + i
+                nc.tensor.matmul(
+                    out=spread[:, i, :],
+                    lhsT=gate_bias_cols[:, x : x + 1].to_broadcast([P, P]),
+                    rhs=identity_bf16[:],
+                    start=True,
+                    stop=True,
+                )
+            nc.scalar.copy(
+                out=gate_bias[:].rearrange("m (n x) -> m n x", x=BIAS_COLS)[:, :, 4 * block : 4 * block + 4],
+                in_=spread[:].rearrange("m x n -> m n x"),
+            )
+
+        def transpose_adjacent(b, half):
+            pairs = adj_rows[b][:].bitcast(F32)
+            flipped = psum_transposes.tile([P, 2, 2, P], F32, name="flipped")
+            in_psum["flipped", b, half] = flipped
+            for r in range(2):
+                for u in range(2):
+                    first = (2 * half + r) * (NODES // 2)
+                    nc.tensor.transpose(flipped[:, r, u, :], pairs[:, first + u : first + NODES // 2 : 2], identity_f32[:])
+
+        def collect_adjacent(b, half):
+            dst = adj[b][0][:].bitcast(F32).rearrange("q (r p u) -> q r p u", r=NODE_TILES, u=2)
+            nc.scalar.copy(
+                out=dst[:, 2 * half : 2 * half + 2],
+                in_=in_psum["flipped", b, half][:].rearrange("q r u p -> q r p u"),
+            )
+
+        def stage1_by_nodes(b, r):
+            bank = psum_stage1.tile([P, CHANNEL_TILES, P], F32, name="bank")
+            in_psum["by_nodes", b, r] = bank
+            for t in range(CHANNEL_TILES):
+                mx_pass(bank[:, t, :], ann[b], P * t, adj[b], P * r, P)
+
+        def msg_by_nodes(b, r):
+            nc.vector.tensor_tensor(
+                out=msg[b][0][:, PACK * P * r : PACK * P * (r + 1)].rearrange("p (j t) -> p j t", t=PACK),
+                in0=in_psum["by_nodes", b, r][:].rearrange("p t j -> p j t"),
+                in1=gc_f32[:].unsqueeze(1).to_broadcast([P, P, PACK]),
+                op=ADD,
+            )
+
+        def stage1_by_channels(b, t):
+            bank = psum_stage1.tile([P, NODES], F32, name="bank")
+            in_psum["by_channels", b, t] = bank
+            mx_pass(bank[:], ann[b], P * t, adj[b], 0, NODES)
+
+        def msg_by_channels(b, t):
+            nc.scalar.activation(
+                out=msg_planes[:, NODES * t : NODES * (t + 1)],
+                in_=in_psum["by_channels", b, t][:],
+                func=IDENTITY,
+                bias=gc_f32[:, t : t + 1],
+                scale=1.0,
+            )
+
+        banks = [(b, g, r) for b in range(GRAPHS) for g in range(GATE_TILES) for r in range(NODE_TILES)]
+
+        def stage2(b, g, r):
+            acc = psum_stage2.tile([P, BANK], F32, name="acc")
+            in_psum["acc", b, g, r] = acc
+            mx_pass(acc[:], msg[b], P * r, w[g], 0, BANK)
+
+        def finish(b, g, r):
+            first = (b * NODE_TILES + r) * GATES + g * BANK
+            nc.vector.tensor_tensor(
+                out=result[:, first : first + BANK],
+                in0=in_psum["acc", b, g, r][:],
+                in1=gate_bias[:, BANK * g : BANK * (g + 1)],
+                op=ADD,
+            )
+            nc.sync.dma_start(out=out_tiles[b, r, :, BANK * g : BANK * (g + 1)], in_=result[:, first : first + BANK])
+
+        nc.sync.dma_start(out=gate_bias_cols[:], in_=gru_b_x.rearrange("(p x) -> p x", x=BIAS_COLS))
+        with nc.allow_non_contiguous_dma(reason="512 values of gc_bias, channel 4 p + t to partition p"):
+            nc.sync.dma_start(out=gc_bf16[:], in_=gc_bias.rearrange("a b (p t) -> p (a b t)", t=CHANNEL_TILES))
+        load_annotations(0)
+        load_adjacent(0, 0, 2)
+        load_adjacent(0, 2, 2)
+        load_weights(0)
+        load_adjacent(1, 0, NODE_TILES)
+        load_annotations(1)
+        load_weights(1)
+        load_weights(2)
+
+        masks.make_identity(nc, identity_f32[:])
+        nc.vector.tensor_copy(out=identity_bf16[:], in_=identity_f32[:])
+        for block in range(BIAS_COLS // 4):
+            spread_gate_bias(block)
+
+        for half in range(2):
+            regroup_annotations(nc.vector.tensor_copy, 0, half)
+        for half in range(2):
+            quantise(ann[0], HALF * half, HALF)
+        for half in range(2):
+            transpose_adjacent(0, half)
+        for half in range(2):
+            collect_adjacent(0, half)
+        for half in range(2):
+            quantise(adj[0], HALF * half, HALF)
+        regroup(nc.vector.tensor_copy, w[0], w_planes[0], 0, HALF)
+        regroup(nc.scalar.copy, w[0], w_planes[0], HALF, HALF)
+        nc.vector.tensor_copy(out=gc_f32[:], in_=gc_bf16[:])
+
+        stage1_by_nodes(0, 0)
+        stage1_by_nodes(0, 1)
+        for half in range(2):
+            transpose_adjacent(1, half)
+        for half in range(2):
+            collect_adjacent(1, half)
+        regroup_annotations(nc.scalar.copy, 1, 0)
+        for half in range(2):
+            regroup(nc.scalar.copy, w[1], w_planes[1], HALF * half, HALF)
+        regroup_annotations(nc.scalar.copy, 1, 1)
+        for piece in range(BANK // P):
+            regroup(gpsimd_copy, w[2], w_planes[2], P * piece, P)
+        msg_by_nodes(0, 0)
+        stage1_by_nodes(0, 2)
+        msg_by_nodes(0, 1)
+        stage1_by_nodes(0, 3)
+        quantise(w[0], 0, BANK)
+        quantise(msg[0], 0, P)
+        msg_by_nodes(0, 2)
+        quantise(msg[0], P, P)
+        msg_by_nodes(0, 3)
+        quantise(msg[0], 2 * P, P)
+        quantise(msg[0], 3 * P, P)
+
+        def start_bank(i):
+            if i < len(banks):
+                stage2(*banks[i])
+
+        def stream(first, stop):
+            for i in range(first, stop):
+                finish(*banks[i])
+                start_bank(i + AHEAD)
+
+        for i in range(AHEAD):
+            start_bank(i)
+
+        finish(*banks[0])
+        for half in range(2):
+            quantise(adj[1], HALF * half, HALF)
+        quantise(ann[1], 0, HALF)
+        start_bank(0 + AHEAD)
+
+        finish(*banks[1])
+        quantise(w[1], 0, BANK)
+        start_bank(1 + AHEAD)
+
+        finish(*banks[2])
+        quantise(ann[1], HALF, HALF)
+        stage1_by_channels(1, 0)
+        stage1_by_channels(1, 1)
+        msg_by_channels(1, 0)
+        msg_by_channels(1, 1)
+        start_bank(2 + AHEAD)
+
+        finish(*banks[3])
+        stage1_by_channels(1, 2)
+        msg_by_channels(1, 2)
+        start_bank(3 + AHEAD)
+
+        finish(*banks[4])
+        stage1_by_channels(1, 3)
+        msg_by_channels(1, 3)
+        for half in range(2):
+            regroup(nc.scalar.copy, msg[1], msg_planes, HALF * half, HALF)
+        start_bank(4 + AHEAD)
+
+        finish(*banks[5])
+        quantise(w[2], 0, BANK)
+        start_bank(5 + AHEAD)
+
+        stream(6, 8)
+
+        finish(*banks[8])
+        quantise(msg[1], 0, HALF)
+        start_bank(8 + AHEAD)
+
+        finish(*banks[9])
+        quantise(msg[1], HALF, HALF)
+        start_bank(9 + AHEAD)
+
+        stream(10, len(banks))

@@ -22,6 +22,8 @@ GATE_TILES = GATES // BANK
 HALF = 256
 BIAS_COLS = GATES // P
 AHEAD = 2
+SHARED = range(11, 21, 3)
+STORE_LAG = 3
 
 FLOPS = 2 * GRAPHS * NODES * NODES * CHANNELS + 2 * GRAPHS * NODES * CHANNELS * GATES
 
@@ -173,15 +175,25 @@ def tile_gatedgraphconvolution_pa_kernel(tc, adjacent, annotations, gc_bias, gru
             in_psum["acc", b, g, r] = acc
             mx_pass(acc[:], msg[b], P * r, w[g], 0, BANK)
 
-        def finish(b, g, r):
+        def result_of(b, g, r):
             first = (b * NODE_TILES + r) * GATES + g * BANK
-            nc.vector.tensor_tensor(
-                out=result[:, first : first + BANK],
-                in0=in_psum["acc", b, g, r][:],
-                in1=gate_bias[:, BANK * g : BANK * (g + 1)],
-                op=ADD,
-            )
-            nc.sync.dma_start(out=out_tiles[b, r, :, BANK * g : BANK * (g + 1)], in_=result[:, first : first + BANK])
+            return result[:, first : first + BANK]
+
+        def store(b, g, r):
+            nc.sync.dma_start(out=out_tiles[b, r, :, BANK * g : BANK * (g + 1)], in_=result_of(b, g, r))
+
+        def finish(i):
+            b, g, r = banks[i]
+            acc = in_psum["acc", b, g, r]
+            bias = gate_bias[:, BANK * g : BANK * (g + 1)]
+            if i in SHARED:
+                nc.scalar.copy(out=result_of(b, g, r), in_=acc[:])
+                nc.gpsimd.tensor_tensor(out=result_of(b, g, r), in0=result_of(b, g, r), in1=bias, op=ADD)
+            else:
+                nc.vector.tensor_tensor(out=result_of(b, g, r), in0=acc[:], in1=bias, op=ADD)
+                store(b, g, r)
+            if i - STORE_LAG in SHARED:
+                store(*banks[i - STORE_LAG])
 
         nc.sync.dma_start(out=gate_bias_cols[:], in_=gru_b_x.rearrange("(p x) -> p x", x=BIAS_COLS))
         with nc.allow_non_contiguous_dma(reason="512 values of gc_bias, channel 4 p + t to partition p"):
@@ -210,8 +222,8 @@ def tile_gatedgraphconvolution_pa_kernel(tc, adjacent, annotations, gc_bias, gru
             collect_adjacent(0, half)
         for half in range(2):
             quantise(adj[0], HALF * half, HALF)
-        regroup(nc.vector.tensor_copy, w[0], w_planes[0], 0, HALF)
-        regroup(nc.scalar.copy, w[0], w_planes[0], HALF, HALF)
+        for half in range(2):
+            regroup(nc.scalar.copy, w[0], w_planes[0], HALF * half, HALF)
         nc.vector.tensor_copy(out=gc_f32[:], in_=gc_bf16[:])
 
         stage1_by_nodes(0, 0)
@@ -244,23 +256,23 @@ def tile_gatedgraphconvolution_pa_kernel(tc, adjacent, annotations, gc_bias, gru
 
         def stream(first, stop):
             for i in range(first, stop):
-                finish(*banks[i])
+                finish(i)
                 start_bank(i + AHEAD)
 
         for i in range(AHEAD):
             start_bank(i)
 
-        finish(*banks[0])
+        finish(0)
         for half in range(2):
             quantise(adj[1], HALF * half, HALF)
         quantise(ann[1], 0, HALF)
         start_bank(0 + AHEAD)
 
-        finish(*banks[1])
+        finish(1)
         quantise(w[1], 0, BANK)
         start_bank(1 + AHEAD)
 
-        finish(*banks[2])
+        finish(2)
         quantise(ann[1], HALF, HALF)
         stage1_by_channels(1, 0)
         stage1_by_channels(1, 1)
@@ -268,29 +280,29 @@ def tile_gatedgraphconvolution_pa_kernel(tc, adjacent, annotations, gc_bias, gru
         msg_by_channels(1, 1)
         start_bank(2 + AHEAD)
 
-        finish(*banks[3])
+        finish(3)
         stage1_by_channels(1, 2)
         msg_by_channels(1, 2)
         start_bank(3 + AHEAD)
 
-        finish(*banks[4])
+        finish(4)
         stage1_by_channels(1, 3)
         msg_by_channels(1, 3)
         for half in range(2):
             regroup(nc.scalar.copy, msg[1], msg_planes, HALF * half, HALF)
         start_bank(4 + AHEAD)
 
-        finish(*banks[5])
+        finish(5)
         quantise(w[2], 0, BANK)
         start_bank(5 + AHEAD)
 
         stream(6, 8)
 
-        finish(*banks[8])
+        finish(8)
         quantise(msg[1], 0, HALF)
         start_bank(8 + AHEAD)
 
-        finish(*banks[9])
+        finish(9)
         quantise(msg[1], HALF, HALF)
         start_bank(9 + AHEAD)
 

@@ -20,9 +20,10 @@ CHANNEL_TILES = CHANNELS // P
 BANK = 512
 GATE_TILES = GATES // BANK
 HALF = 256
+PIECE = 64
 BIAS_COLS = GATES // P
 AHEAD = 2
-SHARED = range(11, 21, 3)
+SHARED = (5, 14)
 STORE_LAG = 3
 
 FLOPS = 2 * GRAPHS * NODES * NODES * CHANNELS + 2 * GRAPHS * NODES * CHANNELS * GATES
@@ -32,8 +33,7 @@ def tile_gatedgraphconvolution_pa_kernel(tc, adjacent, annotations, gc_bias, gru
     nc = tc.nc
     with ExitStack() as ctx:
         sbuf = ctx.enter_context(tc.tile_pool(name="sbuf", bufs=1))
-        psum_transposes = ctx.enter_context(tc.psum_pool(name="psum_transposes", bufs=2))
-        psum_stage1 = ctx.enter_context(tc.psum_pool(name="psum_stage1", bufs=2))
+        psum_stage1 = ctx.enter_context(tc.psum_pool(name="psum_stage1", bufs=4))
         psum_stage2 = ctx.enter_context(tc.psum_pool(name="psum_stage2", bufs=4))
         ctx.enter_context(tc.manual_schedule())
 
@@ -82,6 +82,13 @@ def tile_gatedgraphconvolution_pa_kernel(tc, adjacent, annotations, gc_bias, gru
         def gpsimd_copy(out, in_):
             nc.gpsimd.tensor_scalar(out=out, in0=in_, scalar1=1.0, scalar2=0.0, op0=MULT, op1=ADD)
 
+        def regroup_shared(g, gpsimd_columns):
+            for first in range(0, gpsimd_columns, PIECE):
+                regroup(gpsimd_copy, w[g], w_planes[g], first, PIECE)
+            share = (BANK - gpsimd_columns) // 2
+            for half in range(2):
+                regroup(nc.scalar.copy, w[g], w_planes[g], gpsimd_columns + share * half, share)
+
         def mx_pass(acc, stationary, stationary_first, moving, moving_first, moving_count):
             rows = slice(stationary_first, stationary_first + P)
             cols = slice(moving_first, moving_first + moving_count)
@@ -126,7 +133,7 @@ def tile_gatedgraphconvolution_pa_kernel(tc, adjacent, annotations, gc_bias, gru
 
         def transpose_adjacent(b, half):
             pairs = adj_rows[b][:].bitcast(F32)
-            flipped = psum_transposes.tile([P, 2, 2, P], F32, name="flipped")
+            flipped = psum_stage1.tile([P, 2, 2, P], F32, name="bank")
             in_psum["flipped", b, half] = flipped
             for r in range(2):
                 for u in range(2):
@@ -202,9 +209,9 @@ def tile_gatedgraphconvolution_pa_kernel(tc, adjacent, annotations, gc_bias, gru
         load_adjacent(0, 0, 2)
         load_adjacent(0, 2, 2)
         load_weights(0)
+        load_weights(1)
         load_adjacent(1, 0, NODE_TILES)
         load_annotations(1)
-        load_weights(1)
         load_weights(2)
 
         masks.make_identity(nc, identity_f32[:])
@@ -222,30 +229,26 @@ def tile_gatedgraphconvolution_pa_kernel(tc, adjacent, annotations, gc_bias, gru
             collect_adjacent(0, half)
         for half in range(2):
             quantise(adj[0], HALF * half, HALF)
-        for half in range(2):
-            regroup(nc.scalar.copy, w[0], w_planes[0], HALF * half, HALF)
+        regroup_shared(0, 128)
         nc.vector.tensor_copy(out=gc_f32[:], in_=gc_bf16[:])
 
         stage1_by_nodes(0, 0)
         stage1_by_nodes(0, 1)
-        for half in range(2):
-            transpose_adjacent(1, half)
-        for half in range(2):
-            collect_adjacent(1, half)
-        regroup_annotations(nc.scalar.copy, 1, 0)
-        for half in range(2):
-            regroup(nc.scalar.copy, w[1], w_planes[1], HALF * half, HALF)
-        regroup_annotations(nc.scalar.copy, 1, 1)
-        for piece in range(BANK // P):
-            regroup(gpsimd_copy, w[2], w_planes[2], P * piece, P)
         msg_by_nodes(0, 0)
         stage1_by_nodes(0, 2)
         msg_by_nodes(0, 1)
         stage1_by_nodes(0, 3)
-        quantise(w[0], 0, BANK)
+        regroup_shared(1, 128)
+        for half in range(2):
+            transpose_adjacent(1, half)
+        for half in range(2):
+            collect_adjacent(1, half)
+        for half in range(2):
+            regroup_annotations(nc.scalar.copy, 1, half)
         quantise(msg[0], 0, P)
         msg_by_nodes(0, 2)
         quantise(msg[0], P, P)
+        quantise(w[0], 0, BANK)
         msg_by_nodes(0, 3)
         quantise(msg[0], 2 * P, P)
         quantise(msg[0], 3 * P, P)
@@ -263,47 +266,69 @@ def tile_gatedgraphconvolution_pa_kernel(tc, adjacent, annotations, gc_bias, gru
             start_bank(i)
 
         finish(0)
-        for half in range(2):
-            quantise(adj[1], HALF * half, HALF)
-        quantise(ann[1], 0, HALF)
+        quantise(adj[1], 0, HALF)
+        quantise(adj[1], HALF, HALF)
         start_bank(0 + AHEAD)
-
         finish(1)
         quantise(w[1], 0, BANK)
-        start_bank(1 + AHEAD)
-
-        finish(2)
+        quantise(ann[1], 0, HALF)
         quantise(ann[1], HALF, HALF)
+        start_bank(1 + AHEAD)
+        finish(2)
+        start_bank(2 + AHEAD)
+        finish(3)
+        regroup_shared(2, 256)
+        start_bank(3 + AHEAD)
+        finish(4)
         stage1_by_channels(1, 0)
         stage1_by_channels(1, 1)
+        stage1_by_channels(1, 2)
+        stage1_by_channels(1, 3)
+        quantise(w[2], 0, BANK)
+        start_bank(4 + AHEAD)
+        finish(5)
+        start_bank(5 + AHEAD)
+        finish(6)
         msg_by_channels(1, 0)
         msg_by_channels(1, 1)
-        start_bank(2 + AHEAD)
-
-        finish(3)
-        stage1_by_channels(1, 2)
         msg_by_channels(1, 2)
-        start_bank(3 + AHEAD)
-
-        finish(4)
-        stage1_by_channels(1, 3)
         msg_by_channels(1, 3)
-        for half in range(2):
-            regroup(nc.scalar.copy, msg[1], msg_planes, HALF * half, HALF)
-        start_bank(4 + AHEAD)
-
-        finish(5)
-        quantise(w[2], 0, BANK)
-        start_bank(5 + AHEAD)
-
-        stream(6, 8)
-
+        regroup(nc.scalar.copy, msg[1], msg_planes, 0, HALF)
+        regroup(nc.scalar.copy, msg[1], msg_planes, HALF, HALF)
+        start_bank(6 + AHEAD)
+        finish(7)
+        start_bank(7 + AHEAD)
         finish(8)
-        quantise(msg[1], 0, HALF)
         start_bank(8 + AHEAD)
-
         finish(9)
-        quantise(msg[1], HALF, HALF)
         start_bank(9 + AHEAD)
-
-        stream(10, len(banks))
+        finish(10)
+        quantise(msg[1], 0, HALF)
+        start_bank(10 + AHEAD)
+        finish(11)
+        quantise(msg[1], HALF, HALF)
+        start_bank(11 + AHEAD)
+        finish(12)
+        start_bank(12 + AHEAD)
+        finish(13)
+        start_bank(13 + AHEAD)
+        finish(14)
+        start_bank(14 + AHEAD)
+        finish(15)
+        start_bank(15 + AHEAD)
+        finish(16)
+        start_bank(16 + AHEAD)
+        finish(17)
+        start_bank(17 + AHEAD)
+        finish(18)
+        start_bank(18 + AHEAD)
+        finish(19)
+        start_bank(19 + AHEAD)
+        finish(20)
+        start_bank(20 + AHEAD)
+        finish(21)
+        start_bank(21 + AHEAD)
+        finish(22)
+        start_bank(22 + AHEAD)
+        finish(23)
+        start_bank(23 + AHEAD)

@@ -79,12 +79,15 @@ def tile_gatedgraphconvolution_pa_kernel(tc, adjacent, annotations, gc_bias, gru
             src = ann_planes[b][:].rearrange("q (j i t) -> q t i j", j=PACK, t=CHANNEL_TILES)
             copy(out=dst[:, 2 * half : 2 * half + 2], in_=src[:, 2 * half : 2 * half + 2])
 
-        def gpsimd_copy(out, in_):
-            nc.gpsimd.tensor_scalar(out=out, in0=in_, scalar1=1.0, scalar2=0.0, op0=MULT, op1=ADD)
+        def gpsimd_regroup(mx_operand, planes, first, count):
+            dst = mx_operand[0][:].rearrange("p (c t) -> p c t", t=PACK)
+            src = planes[:].rearrange("p (t c) -> p c t", t=PACK)
+            cols = slice(first, first + count)
+            nc.gpsimd.tensor_scalar(out=dst[:, cols], in0=src[:, cols], scalar1=1.0, scalar2=0.0, op0=MULT, op1=ADD)
 
         def regroup_shared(g, gpsimd_columns):
             for first in range(0, gpsimd_columns, PIECE):
-                regroup(gpsimd_copy, w[g], w_planes[g], first, PIECE)
+                gpsimd_regroup(w[g], w_planes[g], first, PIECE)
             share = (BANK - gpsimd_columns) // 2
             for half in range(2):
                 regroup(nc.scalar.copy, w[g], w_planes[g], gpsimd_columns + share * half, share)

@@ -52,6 +52,7 @@ def tile_gatedgraphconvolution_pa_kernel(tc, adjacent, annotations, gc_bias, gru
         msg = [operand("msg%d" % b, NODES) for b in range(GRAPHS)]
         w = [operand("w%d" % g, BANK) for g in range(GATE_TILES)]
         identity_f32 = sbuf.tile([P, P], F32, name="identity_f32")
+        warm_up = sbuf.tile([P, BANK], BF16, name="warm_up")
         identity_bf16 = sbuf.tile([P, P], BF16, name="identity_bf16")
         gc_bf16 = sbuf.tile([P, CHANNEL_TILES], BF16, name="gc_bf16")
         gc_f32 = sbuf.tile([P, CHANNEL_TILES], F32, name="gc_f32")
@@ -150,6 +151,11 @@ def tile_gatedgraphconvolution_pa_kernel(tc, adjacent, annotations, gc_bias, gru
                 in_=in_psum["flipped", b, half][:].rearrange("q r u p -> q r p u"),
             )
 
+        def keep_warm(passes):
+            for i in range(passes):
+                idle = psum_stage2.tile([P, BANK], F32, name="acc")
+                nc.tensor.matmul(out=idle[:], lhsT=warm_up[:, :P], rhs=warm_up[:], start=True, stop=True)
+
         def stage1_by_nodes(b, r):
             bank = psum_stage1.tile([P, CHANNEL_TILES, P], F32, name="bank")
             in_psum["by_nodes", b, r] = bank
@@ -217,6 +223,8 @@ def tile_gatedgraphconvolution_pa_kernel(tc, adjacent, annotations, gc_bias, gru
         load_annotations(1)
         load_weights(2)
 
+        nc.vector.memset(warm_up[:], 0.0)
+        keep_warm(4)
         masks.make_identity(nc, identity_f32[:])
         nc.vector.tensor_copy(out=identity_bf16[:], in_=identity_f32[:])
         for block in range(BIAS_COLS // 4):
@@ -226,8 +234,9 @@ def tile_gatedgraphconvolution_pa_kernel(tc, adjacent, annotations, gc_bias, gru
             regroup_annotations(nc.vector.tensor_copy, 0, half)
         for half in range(2):
             quantise(ann[0], HALF * half, HALF)
-        for half in range(2):
-            transpose_adjacent(0, half)
+        transpose_adjacent(0, 0)
+        transpose_adjacent(0, 1)
+        keep_warm(2)
         for half in range(2):
             collect_adjacent(0, half)
         for half in range(2):

@@ -212,11 +212,11 @@ def tile_gatedgraphconvolution_pa_kernel(tc, adjacent, annotations, gc_bias, gru
                 store(*banks[i - STORE_LAG])
 
         nc.sync.dma_start(out=gate_bias_cols[:], in_=gru_b_x.rearrange("(p x) -> p x", x=BIAS_COLS))
-        with nc.allow_non_contiguous_dma(reason="512 values of gc_bias, channel 4 p + t to partition p"):
-            nc.sync.dma_start(out=gc_bf16[:], in_=gc_bias.rearrange("a b (p t) -> p (a b t)", t=CHANNEL_TILES))
         load_annotations(0)
         load_adjacent(0, 0, 2)
         load_adjacent(0, 2, 2)
+        with nc.allow_non_contiguous_dma(reason="512 values of gc_bias, channel 4 p + t to partition p"):
+            nc.sync.dma_start(out=gc_bf16[:], in_=gc_bias.rearrange("a b (p t) -> p (a b t)", t=CHANNEL_TILES))
         load_weights(0)
         load_weights(1)
         load_adjacent(1, 0, NODE_TILES)
@@ -224,7 +224,7 @@ def tile_gatedgraphconvolution_pa_kernel(tc, adjacent, annotations, gc_bias, gru
         load_weights(2)
 
         nc.vector.memset(warm_up[:], 0.0)
-        keep_warm(4)
+        keep_warm(2)
         masks.make_identity(nc, identity_f32[:])
         nc.vector.tensor_copy(out=identity_bf16[:], in_=identity_f32[:])
         for block in range(BIAS_COLS // 4):

@@ -20,7 +20,7 @@ CHANNEL_TILES = CHANNELS // P
 BANK = 512
 GATE_TILES = GATES // BANK
 HALF = 256
-PIECE = 64
+PIECE = 32
 BIAS_COLS = GATES // P
 AHEAD = 2
 SHARED = (5, 14)
@@ -204,7 +204,10 @@ def tile_gatedgraphconvolution_pa_kernel(tc, adjacent, annotations, gc_bias, gru
             bias = gate_bias[:, BANK * g : BANK * (g + 1)]
             if i in SHARED:
                 nc.scalar.copy(out=result_of(b, g, r), in_=acc[:])
-                nc.gpsimd.tensor_tensor(out=result_of(b, g, r), in0=result_of(b, g, r), in1=bias, op=ADD)
+                for first in range(0, BANK, 4 * PIECE):
+                    cols = slice(first, first + 4 * PIECE)
+                    piece = result_of(b, g, r)[:, cols]
+                    nc.gpsimd.tensor_tensor(out=piece, in0=piece, in1=bias[:, cols], op=ADD)
             else:
                 nc.vector.tensor_tensor(out=result_of(b, g, r), in0=acc[:], in1=bias, op=ADD)
                 store(b, g, r)
@@ -232,8 +235,7 @@ def tile_gatedgraphconvolution_pa_kernel(tc, adjacent, annotations, gc_bias, gru
 
         for half in range(2):
             regroup_annotations(nc.vector.tensor_copy, 0, half)
-        for half in range(2):
-            quantise(ann[0], HALF * half, HALF)
+        quantise(ann[0], 0, CHANNELS)
         transpose_adjacent(0, 0)
         transpose_adjacent(0, 1)
         keep_warm(2)
@@ -257,13 +259,11 @@ def tile_gatedgraphconvolution_pa_kernel(tc, adjacent, annotations, gc_bias, gru
             collect_adjacent(1, half)
         for half in range(2):
             regroup_annotations(nc.scalar.copy, 1, half)
-        quantise(msg[0], 0, P)
         msg_by_nodes(0, 2)
-        quantise(msg[0], P, P)
-        quantise(w[0], 0, BANK)
+        quantise(msg[0], 0, HALF)
         msg_by_nodes(0, 3)
-        quantise(msg[0], 2 * P, P)
-        quantise(msg[0], 3 * P, P)
+        quantise(w[0], 0, BANK)
+        quantise(msg[0], HALF, HALF)
 
         def start_bank(i):
             if i < len(banks):
@@ -278,13 +278,11 @@ def tile_gatedgraphconvolution_pa_kernel(tc, adjacent, annotations, gc_bias, gru
             start_bank(i)
 
         finish(0)
-        quantise(adj[1], 0, HALF)
-        quantise(adj[1], HALF, HALF)
+        quantise(adj[1], 0, NODES)
         start_bank(0 + AHEAD)
         finish(1)
         quantise(w[1], 0, BANK)
-        quantise(ann[1], 0, HALF)
-        quantise(ann[1], HALF, HALF)
+        quantise(ann[1], 0, CHANNELS)
         start_bank(1 + AHEAD)
         finish(2)
         start_bank(2 + AHEAD)

@@ -151,9 +151,9 @@ def tile_gatedgraphconvolution_pa_kernel(tc, adjacent, annotations, gc_bias, gru
                 in_=in_psum["flipped", b, half][:].rearrange("q r u p -> q r p u"),
             )
 
-        def keep_warm(passes):
+        def keep_warm(pool, name, passes):
             for i in range(passes):
-                idle = psum_stage2.tile([P, BANK], F32, name="acc")
+                idle = pool.tile([P, BANK], F32, name=name)
                 nc.tensor.matmul(out=idle[:], lhsT=warm_up[:, :P], rhs=warm_up[:], start=True, stop=True)
 
         def stage1_by_nodes(b, r):
@@ -227,7 +227,7 @@ def tile_gatedgraphconvolution_pa_kernel(tc, adjacent, annotations, gc_bias, gru
         load_weights(2)
 
         nc.vector.memset(warm_up[:], 0.0)
-        keep_warm(2)
+        keep_warm(psum_stage2, "acc", 2)
         masks.make_identity(nc, identity_f32[:])
         nc.vector.tensor_copy(out=identity_bf16[:], in_=identity_f32[:])
         for block in range(BIAS_COLS // 4):
@@ -235,16 +235,19 @@ def tile_gatedgraphconvolution_pa_kernel(tc, adjacent, annotations, gc_bias, gru
 
         for half in range(2):
             regroup_annotations(nc.vector.tensor_copy, 0, half)
-        quantise(ann[0], 0, CHANNELS)
+        for half in range(2):
+            quantise(ann[0], HALF * half, HALF)
         transpose_adjacent(0, 0)
         transpose_adjacent(0, 1)
-        keep_warm(2)
+        keep_warm(psum_stage2, "acc", 2)
         for half in range(2):
             collect_adjacent(0, half)
         for half in range(2):
             quantise(adj[0], HALF * half, HALF)
-        regroup_shared(0, 128)
         nc.vector.tensor_copy(out=gc_f32[:], in_=gc_bf16[:])
+        regroup(nc.vector.tensor_copy, w[0], w_planes[0], 0, P)
+        for half in range(2):
+            regroup(nc.scalar.copy, w[0], w_planes[0], P + 192 * half, 192)
 
         stage1_by_nodes(0, 0)
         stage1_by_nodes(0, 1)
@@ -261,9 +264,8 @@ def tile_gatedgraphconvolution_pa_kernel(tc, adjacent, annotations, gc_bias, gru
             regroup_annotations(nc.scalar.copy, 1, half)
         msg_by_nodes(0, 2)
         quantise(msg[0], 0, HALF)
-        msg_by_nodes(0, 3)
         quantise(w[0], 0, BANK)
-        quantise(msg[0], HALF, HALF)
+        msg_by_nodes(0, 3)
 
         def start_bank(i):
             if i < len(banks):
@@ -278,12 +280,14 @@ def tile_gatedgraphconvolution_pa_kernel(tc, adjacent, annotations, gc_bias, gru
             start_bank(i)
 
         finish(0)
+        quantise(msg[0], HALF, HALF)
         quantise(adj[1], 0, NODES)
         start_bank(0 + AHEAD)
         finish(1)
         quantise(w[1], 0, BANK)
         quantise(ann[1], 0, CHANNELS)
         start_bank(1 + AHEAD)
+        keep_warm(psum_stage1, "bank", 1)
         finish(2)
         start_bank(2 + AHEAD)
         finish(3)
@@ -312,6 +316,7 @@ def tile_gatedgraphconvolution_pa_kernel(tc, adjacent, annotations, gc_bias, gru
         start_bank(8 + AHEAD)
         finish(9)
         start_bank(9 + AHEAD)
+        keep_warm(psum_stage1, "bank", 2)
         finish(10)
         quantise(msg[1], 0, HALF)
         start_bank(10 + AHEAD)

from contextlib import ExitStack

import concourse.masks as masks
import concourse.mybir as mybir

F32 = mybir.dt.float32
BF16 = mybir.dt.bfloat16
U32 = mybir.dt.uint32
U8 = mybir.dt.uint8
FP8X4 = mybir.dt.float8_e4m3fn_x4
ADD = mybir.AluOpType.add
MULT = mybir.AluOpType.mult
IDENTITY = mybir.ActivationFunctionType.Identity

P = 128
PACK = 4
GRAPHS, NODES, CHANNELS, GATES = 2, 512, 512, 1536
NODE_TILES = NODES // P
CHANNEL_TILES = CHANNELS // P
BANK = 512
GATE_TILES = GATES // BANK
HALF = 256
PIECE = 32
BIAS_COLS = GATES // P
AHEAD = 2
SHARED = (5, 14)
STORE_LAG = 3

FLOPS = 2 * GRAPHS * NODES * NODES * CHANNELS + 2 * GRAPHS * NODES * CHANNELS * GATES


def tile_gatedgraphconvolution_pa_kernel(tc, adjacent, annotations, gc_bias, gru_W, gru_b_x, out):
    nc = tc.nc
    with ExitStack() as ctx:
        sbuf = ctx.enter_context(tc.tile_pool(name="sbuf", bufs=1))
        psum_stage1 = ctx.enter_context(tc.psum_pool(name="psum_stage1", bufs=4))
        psum_stage2 = ctx.enter_context(tc.psum_pool(name="psum_stage2", bufs=4))
        ctx.enter_context(tc.manual_schedule())

        def operand(name, columns):
            grouped = sbuf.tile([P, PACK * columns], BF16, name=name + "_grouped", align_bytes=64)
            words = sbuf.tile([P, columns], U32, name=name + "_words", align_bytes=64)
            scales = sbuf.tile([P, columns], U8, name=name + "_scales", align_bytes=64)
            return grouped, words, scales

        adj_rows = [sbuf.tile([P, NODE_TILES * NODES], BF16, name="adj_rows%d" % b) for b in range(GRAPHS)]
        ann_planes = [sbuf.tile([P, PACK * CHANNELS], BF16, name="ann_planes%d" % b) for b in range(GRAPHS)]
        w_planes = [sbuf.tile([P, PACK * BANK], BF16, name="w_planes%d" % g) for g in range(GATE_TILES)]
        msg_planes = sbuf.tile([P, PACK * NODES], BF16, name="msg_planes")
        adj = [operand("adj%d" % b, NODES) for b in range(GRAPHS)]
        ann = [operand("ann%d" % b, CHANNELS) for b in range(GRAPHS)]
        msg = [operand("msg%d" % b, NODES) for b in range(GRAPHS)]
        w = [operand("w%d" % g, BANK) for g in range(GATE_TILES)]
        identity_f32 = sbuf.tile([P, P], F32, name="identity_f32")
        warm_up = sbuf.tile([P, BANK], BF16, name="warm_up")
        identity_bf16 = sbuf.tile([P, P], BF16, name="identity_bf16")
        gc_bf16 = sbuf.tile([P, CHANNEL_TILES], BF16, name="gc_bf16")
        gc_f32 = sbuf.tile([P, CHANNEL_TILES], F32, name="gc_f32")
        gate_bias_cols = sbuf.tile([P, BIAS_COLS], BF16, name="gate_bias_cols")
        gate_bias = sbuf.tile([P, GATES], F32, name="gate_bias")
        result = sbuf.tile([P, GRAPHS * NODE_TILES * GATES], F32, name="result")
        out_tiles = out.rearrange("(b p r) g -> b r p g", b=GRAPHS, r=NODE_TILES)
        in_psum = {}

        def quantise(mx_operand, first, count):
            grouped, words, scales = mx_operand
            nc.vector.quantize_mx(
                out=words[:, first : first + count].bitcast(FP8X4),
                scales=scales[:, first : first + count],
                in_=grouped[:, PACK * first : PACK * (first + count)],
            )

        def regroup(copy, mx_operand, planes, first, count):
            dst = mx_operand[0][:].rearrange("p (c i t) -> p c t i", i=4, t=PACK)
            src = planes[:].rearrange("p (t c i) -> p c t i", t=PACK, i=4)
            copy(out=dst[:, first // 4 : (first + count) // 4], in_=src[:, first // 4 : (first + count) // 4])

        def regroup_annotations(copy, b, half):
            dst = ann[b][0][:].rearrange("q (t i j) -> q t i j", t=CHANNEL_TILES, j=PACK)
            src = ann_planes[b][:].rearrange("q (j i t) -> q t i j", j=PACK, t=CHANNEL_TILES)
            copy(out=dst[:, 2 * half : 2 * half + 2], in_=src[:, 2 * half : 2 * half + 2])

        def gpsimd_regroup(mx_operand, planes, first, count):
            dst = mx_operand[0][:].rearrange("p (c t) -> p c t", t=PACK)
            src = planes[:].rearrange("p (t c) -> p c t", t=PACK)
            cols = slice(first, first + count)
            nc.gpsimd.tensor_scalar(out=dst[:, cols], in0=src[:, cols], scalar1=1.0, scalar2=0.0, op0=MULT, op1=ADD)

        def regroup_shared(g, gpsimd_columns):
            for first in range(0, gpsimd_columns, PIECE):
                gpsimd_regroup(w[g], w_planes[g], first, PIECE)
            share = (BANK - gpsimd_columns) // 2
            for half in range(2):
                regroup(nc.scalar.copy, w[g], w_planes[g], gpsimd_columns + share * half, share)

        def mx_pass(acc, stationary, stationary_first, moving, moving_first, moving_count):
            rows = slice(stationary_first, stationary_first + P)
            cols = slice(moving_first, moving_first + moving_count)
            nc.tensor.matmul_mx(
                out=acc,
                lhsT=stationary[1][:, rows].bitcast(FP8X4),
                lhsT_scale=stationary[2][:, rows],
                rhs=moving[1][:, cols].bitcast(FP8X4),
                rhs_scale=moving[2][:, cols],
                start=True,
                stop=True,
            )

        def load_adjacent(b, first_tile, tiles):
            cols = slice(first_tile * NODES, (first_tile + tiles) * NODES)
            nc.sync.dma_start(out=adj_rows[b][:, cols], in_=adjacent[b].rearrange("(p r) m -> p (r m)", r=NODE_TILES)[:, cols])

        def load_annotations(b):
            nc.sync.dma_start(out=ann_planes[b][:], in_=annotations[b].rearrange("(q j) c -> q (j c)", j=PACK))

        def load_weights(g):
            nc.sync.dma_start(
                out=w_planes[g][:].rearrange("p (t x) -> p t x", t=PACK),
                in_=gru_W[:, BANK * g : BANK * (g + 1)].rearrange("(p t) x -> p t x", t=PACK),
            )

        def spread_gate_bias(block):
            spread = psum_stage2.tile([P, 4, P], F32, name="acc")
            for i in range(4):
                x = 4 * block + i
                nc.tensor.matmul(
                    out=spread[:, i, :],
                    lhsT=gate_bias_cols[:, x : x + 1].to_broadcast([P, P]),
                    rhs=identity_bf16[:],
                    start=True,
                    stop=True,
                )
            nc.scalar.copy(
                out=gate_bias[:].rearrange("m (n x) -> m n x", x=BIAS_COLS)[:, :, 4 * block : 4 * block + 4],
                in_=spread[:].rearrange("m x n -> m n x"),
            )

        def transpose_adjacent(b, half):
            pairs = adj_rows[b][:].bitcast(F32)
            flipped = psum_stage1.tile([P, 2, 2, P], F32, name="bank")
            in_psum["flipped", b, half] = flipped
            for r in range(2):
                for u in range(2):
                    first = (2 * half + r) * (NODES // 2)
                    nc.tensor.transpose(flipped[:, r, u, :], pairs[:, first + u : first + NODES // 2 : 2], identity_f32[:])

        def collect_adjacent(b, half):
            dst = adj[b][0][:].bitcast(F32).rearrange("q (r p u) -> q r p u", r=NODE_TILES, u=2)
            nc.scalar.copy(
                out=dst[:, 2 * half : 2 * half + 2],
                in_=in_psum["flipped", b, half][:].rearrange("q r u p -> q r p u"),
            )

        def keep_warm(pool, name, passes):
            for i in range(passes):
                idle = pool.tile([P, BANK], F32, name=name)
                nc.tensor.matmul(out=idle[:], lhsT=warm_up[:, :P], rhs=warm_up[:], start=True, stop=True)

        def stage1_by_nodes(b, r):
            bank = psum_stage1.tile([P, CHANNEL_TILES, P], F32, name="bank")
            in_psum["by_nodes", b, r] = bank
            for t in range(CHANNEL_TILES):
                mx_pass(bank[:, t, :], ann[b], P * t, adj[b], P * r, P)

        def msg_by_nodes(b, r):
            nc.vector.tensor_tensor(
                out=msg[b][0][:, PACK * P * r : PACK * P * (r + 1)].rearrange("p (j t) -> p j t", t=PACK),
                in0=in_psum["by_nodes", b, r][:].rearrange("p t j -> p j t"),
                in1=gc_f32[:].unsqueeze(1).to_broadcast([P, P, PACK]),
                op=ADD,
            )

        def stage1_by_channels(b, t):
            bank = psum_stage1.tile([P, NODES], F32, name="bank")
            in_psum["by_channels", b, t] = bank
            mx_pass(bank[:], ann[b], P * t, adj[b], 0, NODES)

        def msg_by_channels(b, t):
            nc.scalar.activation(
                out=msg_planes[:, NODES * t : NODES * (t + 1)],
                in_=in_psum["by_channels", b, t][:],
                func=IDENTITY,
                bias=gc_f32[:, t : t + 1],
                scale=1.0,
            )

        banks = [(b, g, r) for b in range(GRAPHS) for g in range(GATE_TILES) for r in range(NODE_TILES)]

        def stage2(b, g, r):
            acc = psum_stage2.tile([P, BANK], F32, name="acc")
            in_psum["acc", b, g, r] = acc
            mx_pass(acc[:], msg[b], P * r, w[g], 0, BANK)

        def result_of(b, g, r):
            first = (b * NODE_TILES + r) * GATES + g * BANK
            return result[:, first : first + BANK]

        def store(b, g, r):
            nc.sync.dma_start(out=out_tiles[b, r, :, BANK * g : BANK * (g + 1)], in_=result_of(b, g, r))

        def finish(i):
            b, g, r = banks[i]
            acc = in_psum["acc", b, g, r]
            bias = gate_bias[:, BANK * g : BANK * (g + 1)]
            if i in SHARED:
                nc.scalar.copy(out=result_of(b, g, r), in_=acc[:])
                for first in range(0, BANK, 4 * PIECE):
                    cols = slice(first, first + 4 * PIECE)
                    piece = result_of(b, g, r)[:, cols]
                    nc.gpsimd.tensor_tensor(out=piece, in0=piece, in1=bias[:, cols], op=ADD)
            else:
                nc.vector.tensor_tensor(out=result_of(b, g, r), in0=acc[:], in1=bias, op=ADD)
                store(b, g, r)
            if i - STORE_LAG in SHARED:
                store(*banks[i - STORE_LAG])

        nc.sync.dma_start(out=gate_bias_cols[:], in_=gru_b_x.rearrange("(p x) -> p x", x=BIAS_COLS))
        load_annotations(0)
        load_adjacent(0, 0, 2)
        load_adjacent(0, 2, 2)
        with nc.allow_non_contiguous_dma(reason="512 values of gc_bias, channel 4 p + t to partition p"):
            nc.sync.dma_start(out=gc_bf16[:], in_=gc_bias.rearrange("a b (p t) -> p (a b t)", t=CHANNEL_TILES))
        load_weights(0)
        load_weights(1)
        load_adjacent(1, 0, NODE_TILES)
        load_annotations(1)
        load_weights(2)

        nc.vector.memset(warm_up[:], 0.0)
        keep_warm(psum_stage2, "acc", 2)
        masks.make_identity(nc, identity_f32[:])
        nc.vector.tensor_copy(out=identity_bf16[:], in_=identity_f32[:])
        for block in range(BIAS_COLS // 4):
            spread_gate_bias(block)

        for half in range(2):
            regroup_annotations(nc.vector.tensor_copy, 0, half)
        for half in range(2):
            quantise(ann[0], HALF * half, HALF)
        transpose_adjacent(0, 0)
        transpose_adjacent(0, 1)
        keep_warm(psum_stage2, "acc", 2)
        for half in range(2):
            collect_adjacent(0, half)
        for half in range(2):
            quantise(adj[0], HALF * half, HALF)
        nc.vector.tensor_copy(out=gc_f32[:], in_=gc_bf16[:])
        regroup(nc.vector.tensor_copy, w[0], w_planes[0], 0, P)
        for half in range(2):
            regroup(nc.scalar.copy, w[0], w_planes[0], P + 192 * half, 192)

        stage1_by_nodes(0, 0)
        stage1_by_nodes(0, 1)
        msg_by_nodes(0, 0)
        stage1_by_nodes(0, 2)
        msg_by_nodes(0, 1)
        stage1_by_nodes(0, 3)
        regroup_shared(1, 128)
        for half in range(2):
            transpose_adjacent(1, half)
        for half in range(2):
            collect_adjacent(1, half)
        for half in range(2):
            regroup_annotations(nc.scalar.copy, 1, half)
        msg_by_nodes(0, 2)
        quantise(msg[0], 0, HALF)
        quantise(w[0], 0, BANK)
        msg_by_nodes(0, 3)

        def start_bank(i):
            if i < len(banks):
                stage2(*banks[i])

        def stream(first, stop):
            for i in range(first, stop):
                finish(i)
                start_bank(i + AHEAD)

        for i in range(AHEAD):
            start_bank(i)

        finish(0)
        quantise(msg[0], HALF, HALF)
        quantise(adj[1], 0, NODES)
        start_bank(0 + AHEAD)
        finish(1)
        quantise(w[1], 0, BANK)
        quantise(ann[1], 0, CHANNELS)
        start_bank(1 + AHEAD)
        keep_warm(psum_stage1, "bank", 1)
        finish(2)
        start_bank(2 + AHEAD)
        finish(3)
        regroup_shared(2, 256)
        start_bank(3 + AHEAD)
        finish(4)
        stage1_by_channels(1, 0)
        stage1_by_channels(1, 1)
        stage1_by_channels(1, 2)
        stage1_by_channels(1, 3)
        quantise(w[2], 0, BANK)
        start_bank(4 + AHEAD)
        finish(5)
        start_bank(5 + AHEAD)
        finish(6)
        msg_by_channels(1, 0)
        msg_by_channels(1, 1)
        msg_by_channels(1, 2)
        msg_by_channels(1, 3)
        regroup(nc.scalar.copy, msg[1], msg_planes, 0, HALF)
        regroup(nc.scalar.copy, msg[1], msg_planes, HALF, HALF)
        start_bank(6 + AHEAD)
        finish(7)
        start_bank(7 + AHEAD)
        finish(8)
        start_bank(8 + AHEAD)
        finish(9)
        start_bank(9 + AHEAD)
        keep_warm(psum_stage1, "bank", 2)
        finish(10)
        quantise(msg[1], 0, HALF)
        start_bank(10 + AHEAD)
        finish(11)
        quantise(msg[1], HALF, HALF)
        start_bank(11 + AHEAD)
        finish(12)
        start_bank(12 + AHEAD)
        finish(13)
        start_bank(13 + AHEAD)
        finish(14)
        start_bank(14 + AHEAD)
        finish(15)
        start_bank(15 + AHEAD)
        finish(16)
        start_bank(16 + AHEAD)
        finish(17)
        start_bank(17 + AHEAD)
        finish(18)
        start_bank(18 + AHEAD)
        finish(19)
        start_bank(19 + AHEAD)
        finish(20)
        start_bank(20 + AHEAD)
        finish(21)
        start_bank(21 + AHEAD)
        finish(22)
        start_bank(22 + AHEAD)
        finish(23)
        start_bank(23 + AHEAD)
